import numpy as np
import ml_dtypes

BF16 = ml_dtypes.bfloat16


def bf(x):
    return np.asarray(x, np.float32).astype(BF16)


def f32(x):
    return np.asarray(x, np.float32)


def f64(x):
    return np.asarray(x).astype(np.float64)


def striped(idx):
    return np.tile(idx.reshape(-1, 16).T, (8, 1))


B, C, S, D, K, N, O, E = 512, 1024, 1024, 512, 16, 8192, 1024, 2048


def relu(v):
    return np.maximum(v, 0.0)


def setup_inputs():
    std = np.sqrt(2.0 / K)
    return {
        "x": f32(np.random.standard_normal((C, S))),
        "wp": f32(std * np.random.standard_normal((1, N))),
        "wn": f32(std * np.random.standard_normal((1, N))),
        "bp": f32(0.1 * np.random.standard_normal((D, 1))),
        "bn": f32(0.1 * np.random.standard_normal((D, 1))),
        "fcp_w": bf(np.random.standard_normal((D, O)) / np.sqrt(D)),
        "fcp_b": f32(0.1 * np.random.standard_normal((O, 1))),
        "fcn_w": bf(np.random.standard_normal((D, O)) / np.sqrt(D)),
        "fcn_b": f32(0.1 * np.random.standard_normal((O, 1))),
        "fc3_w": bf(np.random.standard_normal((E, O)) / np.sqrt(E)),
        "fc3_b": f32(0.1 * np.random.standard_normal((O, 1))),
        "offs": striped(np.concatenate([np.random.permutation(S)[:D] for _ in range(K)])),
    }


def reference(x, wp, wn, bp, bn, fcp_w, fcp_b, fcn_w, fcn_b, fc3_w, fc3_b, offs):
    idx = offs[:16].T.reshape(-1)
    picked = f64(x)[:, idx]
    ap = (picked[:B] * f64(wp)).reshape(B, K, D).sum(axis=1)
    an = (picked[B:] * f64(wn)).reshape(B, K, D).sum(axis=1)
    hp = relu(ap.T + f64(bp))
    hn = relu(an.T + f64(bn))
    yp = f64(fcp_w).T @ hp + f64(fcp_b)
    yn = f64(fcn_w).T @ hn + f64(fcn_b)
    u = relu(np.concatenate([yp, yn], axis=0))
    return f64(fc3_w).T @ u + f64(fc3_b)

@@ -1,0 +1,167 @@
+import concourse.mybir as mybir
+from concourse.masks import make_identity
+
+F32 = mybir.dt.float32
+BF16 = mybir.dt.bfloat16
+U16 = mybir.dt.uint16
+MULT = mybir.AluOpType.mult
+RELU = mybir.ActivationFunctionType.Relu
+IDENTITY = mybir.ActivationFunctionType.Identity
+
+P = 128
+SAMPLES = 512
+IN_NODES = 1024
+OUT_NODES = 512
+NEIGHBOURS = 16
+LIST = NEIGHBOURS * OUT_NODES
+HEAD = 1024
+CHANNELS = 2
+
+PIECE = 1024
+PIECES = LIST // PIECE
+NODE_BLOCKS = OUT_NODES // P
+HEAD_BLOCKS = HEAD // P
+JOINT_BLOCKS = CHANNELS * HEAD_BLOCKS
+STEPS = CHANNELS * SAMPLES // P
+assert PIECES == HEAD_BLOCKS
+
+FLOPS = 2 * CHANNELS * SAMPLES * LIST + 2 * SAMPLES * (CHANNELS * OUT_NODES * HEAD + CHANNELS * HEAD * HEAD)
+
+
+def tile_lcnchannelstack_b_kernel(
+    tc, x, wp, wn, bp, bn, fcp_w, fcp_b, fcn_w, fcn_b, fc3_w, fc3_b, offs, out
+):
+    nc = tc.nc
+    with (
+        tc.tile_pool(name="held", bufs=1) as held,
+        tc.tile_pool(name="products", bufs=6) as products,
+        tc.tile_pool(name="acts", bufs=2) as acts,
+        tc.tile_pool(name="results", bufs=4) as results,
+        tc.psum_pool(name="node_psum", bufs=2) as node_psum,
+        tc.psum_pool(name="head_psum", bufs=2) as head_psum,
+        tc.psum_pool(name="joint_psum", bufs=2) as joint_psum,
+    ):
+        offsets = held.tile([P, LIST // 16], U16, name="offsets")
+        identity = held.tile([P, P], F32, name="identity")
+        x_tiles = [held.tile([P, IN_NODES], F32, name=f"x{s}") for s in range(STEPS)]
+        w_tiles = [
+            [held.tile([P, PIECE], F32, name=f"w{c}_{j}") for j in range(PIECES)]
+            for c in range(CHANNELS)
+        ]
+        node_bias = [held.tile([P, NODE_BLOCKS], F32, name=f"node_bias{c}") for c in range(CHANNELS)]
+        head_w = [held.tile([P, NODE_BLOCKS, HEAD], BF16, name=f"head_w{c}") for c in range(CHANNELS)]
+        head_bias = [held.tile([P, HEAD_BLOCKS], F32, name=f"head_bias{c}") for c in range(CHANNELS)]
+        joint_w = held.tile([P, JOINT_BLOCKS, HEAD], BF16, name="joint_w")
+        joint_bias = held.tile([P, HEAD_BLOCKS], F32, name="joint_bias")
+
+        make_identity(nc, identity[:])
+
+        def load_x(queue, s):
+            row = (s % CHANNELS) * SAMPLES + (s // CHANNELS) * P
+            queue.dma_start(x_tiles[s][:], x[row : row + P, :])
+
+        def load_column(tile, vector):
+            nc.sync.dma_start(tile[:], vector.rearrange("(a p) o -> p (a o)", p=P))
+
+        def load_rows(queue, tile, matrix):
+            queue.dma_start(tile[:], matrix.rearrange("(a p) o -> p a o", p=P))
+
+        nc.sync.dma_start(offsets[:], offs)
+        load_x(nc.sync, 0)
+        load_x(nc.sync, 1)
+        with nc.allow_non_contiguous_dma(reason="bias vectors, one float32 to a partition"):
+            load_column(node_bias[0], bp)
+            load_column(node_bias[1], bn)
+            load_column(head_bias[0], fcp_b)
+            load_column(head_bias[1], fcn_b)
+            load_column(joint_bias, fc3_b)
+        load_rows(nc.sync, head_w[0], fcp_w)
+        load_rows(nc.sync, head_w[1], fcn_w)
+        load_x(nc.sync, 2)
+        load_x(nc.sync, 3)
+
+        for c, w in enumerate((wp, wn)):
+            w_row = w.rearrange("o n -> (o n)")
+            for j in range(PIECES):
+                nc.scalar.dma_start(
+                    w_tiles[c][j][:], w_row[j * PIECE : (j + 1) * PIECE].partition_broadcast(P)
+                )
+        load_rows(nc.scalar, joint_w, fc3_w)
+        for s in range(4, STEPS):
+            load_x(nc.scalar, s)
+
+        node_sums = {}
+        hidden = {}
+        joint_in = {}
+
+        def look_up(s, j):
+            if j == 0:
+                node_sums[s] = node_psum.tile([P, NODE_BLOCKS, P], F32, name="node_sum")
+            prod = products.tile([P, PIECE], F32, name="prod")
+            nc.vector.tensor_tensor(
+                prod[:],
+                x_tiles[s][:].indirect(offsets[:, j * PIECE // 16 : (j + 1) * PIECE // 16]),
+                w_tiles[s % CHANNELS][j][:],
+                MULT,
+            )
+            blocks = PIECE // P
+            for i in range(blocks):
+                nc.tensor.matmul(
+                    node_sums[s][:, i % NODE_BLOCKS, :],
+                    lhsT=prod[:, i * P : (i + 1) * P],
+                    rhs=identity[:],
+                    start=(j == 0 and i == 0),
+                    stop=(j == PIECES - 1 and i == blocks - 1),
+                )
+
+        def activate_nodes(s):
+            hidden[s] = acts.tile([P, NODE_BLOCKS, P], BF16, name="hidden")
+            for a in range(NODE_BLOCKS):
+                nc.scalar.activation(
+                    hidden[s][:, a, :],
+                    node_sums[s][:, a, :],
+                    RELU,
+                    bias=node_bias[s % CHANNELS][:, a : a + 1],
+                )
+
+        def head_block(s, m):
+            c, pair = s % CHANNELS, s // CHANNELS
+            if c == 0 and m == 0:
+                joint_in[pair] = acts.tile([P, JOINT_BLOCKS, P], BF16, name="joint_in")
+            y = head_psum.tile([P, P], F32, name="y")
+            for a in range(NODE_BLOCKS):
+                nc.tensor.matmul(
+                    y[:],
+                    lhsT=head_w[c][:, a, m * P : (m + 1) * P],
+                    rhs=hidden[s][:, a, :],
+                    start=(a == 0),
+                    stop=(a == NODE_BLOCKS - 1),
+                )
+            nc.scalar.activation(
+                joint_in[pair][:, c * HEAD_BLOCKS + m, :], y[:], RELU, bias=head_bias[c][:, m : m + 1]
+            )
+
+        def joint_block(pair, m):
+            z = joint_psum.tile([P, P], F32, name="z")
+            for e in range(JOINT_BLOCKS):
+                nc.tensor.matmul(
+                    z[:],
+                    lhsT=joint_w[:, e, m * P : (m + 1) * P],
+                    rhs=joint_in[pair][:, e, :],
+                    start=(e == 0),
+                    stop=(e == JOINT_BLOCKS - 1),
+                )
+            result = results.tile([P, P], F32, name="result")
+            nc.scalar.activation(result[:], z[:], IDENTITY, bias=joint_bias[:, m : m + 1])
+            nc.sync.dma_start(out[m * P : (m + 1) * P, pair * P : (pair + 1) * P], result[:])
+
+        for t in range(STEPS + 2):
+            for j in range(PIECES):
+                if t < STEPS:
+                    look_up(t, j)
+                if 0 <= t - 1 < STEPS:
+                    head_block(t - 1, j)
+                if t - 2 >= 0 and (t - 2) % CHANNELS == CHANNELS - 1:
+                    joint_block((t - 2) // CHANNELS, j)
+            if t < STEPS:
+                activate_nodes(t)

@@ -110,6 +110,7 @@ def tile_lcnchannelstack_b_kernel(
                     node_sums[s][:, i % NODE_BLOCKS, :],
                     lhsT=prod[:, i * P : (i + 1) * P],
                     rhs=identity[:],
+                    is_transpose=True,
                     start=(j == 0 and i == 0),
                     stop=(j == PIECES - 1 and i == blocks - 1),
                 )

@@ -23,6 +23,8 @@ NODE_BLOCKS = OUT_NODES // P
 HEAD_BLOCKS = HEAD // P
 JOINT_BLOCKS = CHANNELS * HEAD_BLOCKS
 STEPS = CHANNELS * SAMPLES // P
+BANK_BLOCKS = 4
+OUT_BANKS = HEAD_BLOCKS // BANK_BLOCKS
 assert PIECES == HEAD_BLOCKS
 
 FLOPS = 2 * CHANNELS * SAMPLES * LIST + 2 * SAMPLES * (CHANNELS * OUT_NODES * HEAD + CHANNELS * HEAD * HEAD)
@@ -36,7 +38,7 @@ def tile_lcnchannelstack_b_kernel(
         tc.tile_pool(name="held", bufs=1) as held,
         tc.tile_pool(name="products", bufs=6) as products,
         tc.tile_pool(name="acts", bufs=2) as acts,
-        tc.tile_pool(name="results", bufs=4) as results,
+        tc.tile_pool(name="results", bufs=2) as results,
         tc.psum_pool(name="node_psum", bufs=2) as node_psum,
         tc.psum_pool(name="head_psum", bufs=2) as head_psum,
         tc.psum_pool(name="joint_psum", bufs=2) as joint_psum,
@@ -93,6 +95,7 @@ def tile_lcnchannelstack_b_kernel(
         node_sums = {}
         hidden = {}
         joint_in = {}
+        joint_sums = {}
 
         def look_up(s, j):
             if j == 0:
@@ -142,27 +145,48 @@ def tile_lcnchannelstack_b_kernel(
                 joint_in[pair][:, c * HEAD_BLOCKS + m, :], y[:], RELU, bias=head_bias[c][:, m : m + 1]
             )
 
-        def joint_block(pair, m):
-            z = joint_psum.tile([P, P], F32, name="z")
-            for e in range(JOINT_BLOCKS):
+        def joint_part(s, e_in_head):
+            c, pair = s % CHANNELS, s // CHANNELS
+            e = c * HEAD_BLOCKS + e_in_head
+            if e == 0:
+                joint_sums[pair] = [
+                    joint_psum.tile([P, BANK_BLOCKS, P], F32, name=f"joint_sum{bank}") for bank in range(OUT_BANKS)
+                ]
+            for m in range(HEAD_BLOCKS):
                 nc.tensor.matmul(
-                    z[:],
+                    joint_sums[pair][m // BANK_BLOCKS][:, m % BANK_BLOCKS, :],
                     lhsT=joint_w[:, e, m * P : (m + 1) * P],
                     rhs=joint_in[pair][:, e, :],
-                    start=(e == 0),
-                    stop=(e == JOINT_BLOCKS - 1),
+                    start=(e == 0 and m % BANK_BLOCKS == 0),
+                    stop=(e == JOINT_BLOCKS - 1 and m % BANK_BLOCKS == BANK_BLOCKS - 1),
                 )
-            result = results.tile([P, P], F32, name="result")
-            nc.scalar.activation(result[:], z[:], IDENTITY, bias=joint_bias[:, m : m + 1])
-            nc.sync.dma_start(out[m * P : (m + 1) * P, pair * P : (pair + 1) * P], result[:])
 
-        for t in range(STEPS + 2):
-            for j in range(PIECES):
-                if t < STEPS:
-                    look_up(t, j)
-                if 0 <= t - 1 < STEPS:
-                    head_block(t - 1, j)
-                if t - 2 >= 0 and (t - 2) % CHANNELS == CHANNELS - 1:
-                    joint_block((t - 2) // CHANNELS, j)
-            if t < STEPS:
-                activate_nodes(t)
+        def store_pair(pair):
+            out_blocks = out.rearrange("(m p) r -> p m r", p=P)
+            result = results.tile([P, HEAD_BLOCKS, P], F32, name="result")
+            for m in range(HEAD_BLOCKS):
+                nc.scalar.activation(
+                    result[:, m, :],
+                    joint_sums[pair][m // BANK_BLOCKS][:, m % BANK_BLOCKS, :],
+                    IDENTITY,
+                    bias=joint_bias[:, m : m + 1],
+                )
+            for bank in range(OUT_BANKS):
+                of_bank = slice(bank * BANK_BLOCKS, (bank + 1) * BANK_BLOCKS)
+                nc.sync.dma_start(out_blocks[:, of_bank, pair * P : (pair + 1) * P], result[:, of_bank, :])
+
+        look_ups = STEPS * PIECES
+        head_lag = PIECES
+        joint_lag = PIECES + 1
+        for turn in range(look_ups + joint_lag):
+            if turn < look_ups:
+                look_up(turn // PIECES, turn % PIECES)
+            if 0 <= turn - head_lag < look_ups:
+                head_block((turn - head_lag) // PIECES, (turn - head_lag) % PIECES)
+            if turn - joint_lag >= 0:
+                s, e_in_head = (turn - joint_lag) // PIECES, (turn - joint_lag) % PIECES
+                joint_part(s, e_in_head)
+                if s % CHANNELS == CHANNELS - 1 and e_in_head == HEAD_BLOCKS - 1:
+                    store_pair(s // CHANNELS)
+            if turn < look_ups and turn % PIECES == PIECES - 1:
+                activate_nodes(turn // PIECES)

@@ -19,15 +19,25 @@ CHANNELS = 2
 
 PIECE = 1024
 PIECES = LIST // PIECE
+FIRST_CUTS = (256, 256, 512)
+assert sum(FIRST_CUTS) == PIECE
 NODE_BLOCKS = OUT_NODES // P
 HEAD_BLOCKS = HEAD // P
 JOINT_BLOCKS = CHANNELS * HEAD_BLOCKS
 STEPS = CHANNELS * SAMPLES // P
-BANK_BLOCKS = 4
-OUT_BANKS = HEAD_BLOCKS // BANK_BLOCKS
-assert PIECES == HEAD_BLOCKS
+FULL_BANK = 4
+assert NODE_BLOCKS == FULL_BANK
+HEAD_BANKS = HEAD_BLOCKS // FULL_BANK
+OUT_BANKS = 4
+BANK_BLOCKS = HEAD_BLOCKS // OUT_BANKS
+EARLY_BANKS = OUT_BANKS // 2
 
 FLOPS = 2 * CHANNELS * SAMPLES * LIST + 2 * SAMPLES * (CHANNELS * OUT_NODES * HEAD + CHANNELS * HEAD * HEAD)
+
+
+def cuts(s, j):
+    widths = FIRST_CUTS if (s, j) == (0, 0) else (PIECE,)
+    return [(sum(widths[:i]), width) for i, width in enumerate(widths)]
 
 
 def tile_lcnchannelstack_b_kernel(
@@ -38,10 +48,10 @@ def tile_lcnchannelstack_b_kernel(
         tc.tile_pool(name="held", bufs=1) as held,
         tc.tile_pool(name="products", bufs=6) as products,
         tc.tile_pool(name="acts", bufs=2) as acts,
-        tc.tile_pool(name="results", bufs=2) as results,
+        tc.tile_pool(name="results", bufs=OUT_BANKS) as results,
         tc.psum_pool(name="node_psum", bufs=2) as node_psum,
         tc.psum_pool(name="head_psum", bufs=2) as head_psum,
-        tc.psum_pool(name="joint_psum", bufs=2) as joint_psum,
+        tc.psum_pool(name="joint_psum", bufs=1) as joint_psum,
     ):
         offsets = held.tile([P, LIST // 16], U16, name="offsets")
         identity = held.tile([P, P], F32, name="identity")
@@ -58,39 +68,45 @@ def tile_lcnchannelstack_b_kernel(
 
         make_identity(nc, identity[:])
 
-        def load_x(queue, s):
+        def x_rows(s):
             row = (s % CHANNELS) * SAMPLES + (s // CHANNELS) * P
-            queue.dma_start(x_tiles[s][:], x[row : row + P, :])
+            return x[row : row + P, :]
 
-        def load_column(tile, vector):
-            nc.sync.dma_start(tile[:], vector.rearrange("(a p) o -> p (a o)", p=P))
+        def repeated(w, first, entries):
+            return w.rearrange("o n -> (o n)")[first : first + entries].partition_broadcast(P)
 
-        def load_rows(queue, tile, matrix):
-            queue.dma_start(tile[:], matrix.rearrange("(a p) o -> p a o", p=P))
+        def column(vector):
+            return vector.rearrange("(a p) o -> p (a o)", p=P)
+
+        def row_blocks(matrix):
+            return matrix.rearrange("(a p) o -> p a o", p=P)
+
+        half = IN_NODES // 2
+        loads = [(x_tiles[0][:, :half], x_rows(0)[:, :half]), (x_tiles[0][:, half:], x_rows(0)[:, half:])]
+        loads.extend((w_tiles[0][0][:, start : start + width], repeated(wp, start, width)) for start, width in cuts(0, 0))
+        loads.extend((w_tiles[0][j][:], repeated(wp, j * PIECE, PIECE)) for j in range(1, PIECES))
+        loads.append((x_tiles[1][:], x_rows(1)))
+        loads.extend((w_tiles[1][j][:], repeated(wn, j * PIECE, PIECE)) for j in range(PIECES))
+        loads.extend(
+            [
+                (node_bias[0][:], column(bp)),
+                (head_bias[0][:], column(fcp_b)),
+                (head_w[0][:], row_blocks(fcp_w)),
+                (joint_w[:, :HEAD_BLOCKS, :], row_blocks(fc3_w[:HEAD, :])),
+                (x_tiles[2][:], x_rows(2)),
+                (node_bias[1][:], column(bn)),
+                (head_bias[1][:], column(fcn_b)),
+                (head_w[1][:], row_blocks(fcn_w)),
+                (joint_w[:, HEAD_BLOCKS:, :], row_blocks(fc3_w[HEAD:, :])),
+                (joint_bias[:], column(fc3_b)),
+            ]
+        )
+        loads.extend((x_tiles[s][:], x_rows(s)) for s in range(3, STEPS))
 
         nc.sync.dma_start(offsets[:], offs)
-        load_x(nc.sync, 0)
-        load_x(nc.sync, 1)
         with nc.allow_non_contiguous_dma(reason="bias vectors, one float32 to a partition"):
-            load_column(node_bias[0], bp)
-            load_column(node_bias[1], bn)
-            load_column(head_bias[0], fcp_b)
-            load_column(head_bias[1], fcn_b)
-            load_column(joint_bias, fc3_b)
-        load_rows(nc.sync, head_w[0], fcp_w)
-        load_rows(nc.sync, head_w[1], fcn_w)
-        load_x(nc.sync, 2)
-        load_x(nc.sync, 3)
-
-        for c, w in enumerate((wp, wn)):
-            w_row = w.rearrange("o n -> (o n)")
-            for j in range(PIECES):
-                nc.scalar.dma_start(
-                    w_tiles[c][j][:], w_row[j * PIECE : (j + 1) * PIECE].partition_broadcast(P)
-                )
-        load_rows(nc.scalar, joint_w, fc3_w)
-        for s in range(4, STEPS):
-            load_x(nc.scalar, s)
+            for i, (part, source) in enumerate(loads):
+                (nc.scalar, nc.sync)[i % 2].dma_start(part, source)
 
         node_sums = {}
         hidden = {}
@@ -100,23 +116,25 @@ def tile_lcnchannelstack_b_kernel(
         def look_up(s, j):
             if j == 0:
                 node_sums[s] = node_psum.tile([P, NODE_BLOCKS, P], F32, name="node_sum")
-            prod = products.tile([P, PIECE], F32, name="prod")
-            nc.vector.tensor_tensor(
-                prod[:],
-                x_tiles[s][:].indirect(offsets[:, j * PIECE // 16 : (j + 1) * PIECE // 16]),
-                w_tiles[s % CHANNELS][j][:],
-                MULT,
-            )
-            blocks = PIECE // P
-            for i in range(blocks):
-                nc.tensor.matmul(
-                    node_sums[s][:, i % NODE_BLOCKS, :],
-                    lhsT=prod[:, i * P : (i + 1) * P],
-                    rhs=identity[:],
-                    is_transpose=True,
-                    start=(j == 0 and i == 0),
-                    stop=(j == PIECES - 1 and i == blocks - 1),
+            for start, width in cuts(s, j):
+                first = j * PIECE + start
+                prod = products.tile([P, PIECE], F32, name="prod")
+                nc.vector.tensor_tensor(
+                    prod[:, :width],
+                    x_tiles[s][:].indirect(offsets[:, first // 16 : (first + width) // 16]),
+                    w_tiles[s % CHANNELS][j][:, start : start + width],
+                    MULT,
                 )
+                for i in range(width // P):
+                    entry = first + i * P
+                    nc.tensor.matmul(
+                        node_sums[s][:, entry // P % NODE_BLOCKS, :],
+                        lhsT=prod[:, i * P : (i + 1) * P],
+                        rhs=identity[:],
+                        is_transpose=True,
+                        start=(entry == 0),
+                        stop=(entry == LIST - P),
+                    )
 
         def activate_nodes(s):
             hidden[s] = acts.tile([P, NODE_BLOCKS, P], BF16, name="hidden")
@@ -128,31 +146,35 @@ def tile_lcnchannelstack_b_kernel(
                     bias=node_bias[s % CHANNELS][:, a : a + 1],
                 )
 
-        def head_block(s, m):
+        def head_bank(s, bank):
             c, pair = s % CHANNELS, s // CHANNELS
-            if c == 0 and m == 0:
+            if c == 0 and bank == 0:
                 joint_in[pair] = acts.tile([P, JOINT_BLOCKS, P], BF16, name="joint_in")
-            y = head_psum.tile([P, P], F32, name="y")
+            y = head_psum.tile([P, FULL_BANK, P], F32, name="y")
             for a in range(NODE_BLOCKS):
-                nc.tensor.matmul(
-                    y[:],
-                    lhsT=head_w[c][:, a, m * P : (m + 1) * P],
-                    rhs=hidden[s][:, a, :],
-                    start=(a == 0),
-                    stop=(a == NODE_BLOCKS - 1),
+                for i in range(FULL_BANK):
+                    m = bank * FULL_BANK + i
+                    nc.tensor.matmul(
+                        y[:, i, :],
+                        lhsT=head_w[c][:, a, m * P : (m + 1) * P],
+                        rhs=hidden[s][:, a, :],
+                        start=(a == 0 and i == 0),
+                        stop=(a == NODE_BLOCKS - 1 and i == FULL_BANK - 1),
+                    )
+            for i in range(FULL_BANK):
+                m = bank * FULL_BANK + i
+                nc.scalar.activation(
+                    joint_in[pair][:, c * HEAD_BLOCKS + m, :], y[:, i, :], RELU, bias=head_bias[c][:, m : m + 1]
                 )
-            nc.scalar.activation(
-                joint_in[pair][:, c * HEAD_BLOCKS + m, :], y[:], RELU, bias=head_bias[c][:, m : m + 1]
-            )
 
-        def joint_part(s, e_in_head):
+        def joint_part(s, e_in_head, banks):
             c, pair = s % CHANNELS, s // CHANNELS
             e = c * HEAD_BLOCKS + e_in_head
             if e == 0:
                 joint_sums[pair] = [
                     joint_psum.tile([P, BANK_BLOCKS, P], F32, name=f"joint_sum{bank}") for bank in range(OUT_BANKS)
                 ]
-            for m in range(HEAD_BLOCKS):
+            for m in range(banks.start * BANK_BLOCKS, banks.stop * BANK_BLOCKS):
                 nc.tensor.matmul(
                     joint_sums[pair][m // BANK_BLOCKS][:, m % BANK_BLOCKS, :],
                     lhsT=joint_w[:, e, m * P : (m + 1) * P],
@@ -161,32 +183,45 @@ def tile_lcnchannelstack_b_kernel(
                     stop=(e == JOINT_BLOCKS - 1 and m % BANK_BLOCKS == BANK_BLOCKS - 1),
                 )
 
-        def store_pair(pair):
+        def store_bank(pair, bank):
             out_blocks = out.rearrange("(m p) r -> p m r", p=P)
-            result = results.tile([P, HEAD_BLOCKS, P], F32, name="result")
-            for m in range(HEAD_BLOCKS):
+            result = results.tile([P, BANK_BLOCKS, P], F32, name="result")
+            for i in range(BANK_BLOCKS):
+                m = bank * BANK_BLOCKS + i
                 nc.scalar.activation(
-                    result[:, m, :],
-                    joint_sums[pair][m // BANK_BLOCKS][:, m % BANK_BLOCKS, :],
-                    IDENTITY,
-                    bias=joint_bias[:, m : m + 1],
+                    result[:, i, :], joint_sums[pair][bank][:, i, :], IDENTITY, bias=joint_bias[:, m : m + 1]
                 )
-            for bank in range(OUT_BANKS):
-                of_bank = slice(bank * BANK_BLOCKS, (bank + 1) * BANK_BLOCKS)
-                nc.sync.dma_start(out_blocks[:, of_bank, pair * P : (pair + 1) * P], result[:, of_bank, :])
+            of_bank = slice(bank * BANK_BLOCKS, (bank + 1) * BANK_BLOCKS)
+            nc.sync.dma_start(out_blocks[:, of_bank, pair * P : (pair + 1) * P], result[:])
 
-        look_ups = STEPS * PIECES
-        head_lag = PIECES
-        joint_lag = PIECES + 1
-        for turn in range(look_ups + joint_lag):
-            if turn < look_ups:
-                look_up(turn // PIECES, turn % PIECES)
-            if 0 <= turn - head_lag < look_ups:
-                head_block((turn - head_lag) // PIECES, (turn - head_lag) % PIECES)
-            if turn - joint_lag >= 0:
-                s, e_in_head = (turn - joint_lag) // PIECES, (turn - joint_lag) % PIECES
-                joint_part(s, e_in_head)
-                if s % CHANNELS == CHANNELS - 1 and e_in_head == HEAD_BLOCKS - 1:
-                    store_pair(s // CHANNELS)
-            if turn < look_ups and turn % PIECES == PIECES - 1:
-                activate_nodes(turn // PIECES)
+        def dense_share(s, j):
+            pair = s // CHANNELS
+            first_joint = PIECES - OUT_BANKS
+            first_head = first_joint - HEAD_BANKS
+            if first_head <= j < first_joint:
+                head_bank(s, j - first_head)
+            elif j >= first_joint and s % CHANNELS < CHANNELS - 1:
+                quarter = HEAD_BLOCKS // OUT_BANKS
+                for e_in_head in range((j - first_joint) * quarter, (j - first_joint + 1) * quarter):
+                    joint_part(s, e_in_head, range(OUT_BANKS))
+            elif first_joint <= j < first_joint + EARLY_BANKS:
+                half = HEAD_BLOCKS // EARLY_BANKS
+                for e_in_head in range((j - first_joint) * half, (j - first_joint + 1) * half):
+                    joint_part(s, e_in_head, range(EARLY_BANKS))
+                if j == first_joint + EARLY_BANKS - 1:
+                    for bank in range(EARLY_BANKS):
+                        store_bank(pair, bank)
+            elif j >= first_joint + EARLY_BANKS:
+                bank = j - first_joint
+                for e_in_head in range(HEAD_BLOCKS):
+                    joint_part(s, e_in_head, range(bank, bank + 1))
+                store_bank(pair, bank)
+
+        for s in range(STEPS + 1):
+            for j in range(PIECES):
+                if s < STEPS:
+                    look_up(s, j)
+                if s > 0:
+                    dense_share(s - 1, j)
+            if s < STEPS:
+                activate_nodes(s)

@@ -21,12 +21,15 @@ PIECE = 1024
 PIECES = LIST // PIECE
 FIRST_CUTS = (256, 256, 512)
 assert sum(FIRST_CUTS) == PIECE
+NODE_HALVES = 2
+FINE_NEIGHBOURS = 6
+FINE_PIECES = FINE_NEIGHBOURS * OUT_NODES // PIECE
 NODE_BLOCKS = OUT_NODES // P
 HEAD_BLOCKS = HEAD // P
 JOINT_BLOCKS = CHANNELS * HEAD_BLOCKS
 STEPS = CHANNELS * SAMPLES // P
+HALF_BLOCKS = NODE_BLOCKS // NODE_HALVES
 FULL_BANK = 4
-assert NODE_BLOCKS == FULL_BANK
 HEAD_BANKS = HEAD_BLOCKS // FULL_BANK
 OUT_BANKS = 4
 BANK_BLOCKS = HEAD_BLOCKS // OUT_BANKS
@@ -35,22 +38,17 @@ EARLY_BANKS = OUT_BANKS // 2
 FLOPS = 2 * CHANNELS * SAMPLES * LIST + 2 * SAMPLES * (CHANNELS * OUT_NODES * HEAD + CHANNELS * HEAD * HEAD)
 
 
-def cuts(s, j):
-    widths = FIRST_CUTS if (s, j) == (0, 0) else (PIECE,)
-    return [(sum(widths[:i]), width) for i, width in enumerate(widths)]
-
-
 def tile_lcnchannelstack_b_kernel(
     tc, x, wp, wn, bp, bn, fcp_w, fcp_b, fcn_w, fcn_b, fc3_w, fc3_b, offs, out
 ):
     nc = tc.nc
     with (
         tc.tile_pool(name="held", bufs=1) as held,
-        tc.tile_pool(name="products", bufs=6) as products,
+        tc.tile_pool(name="products", bufs=10) as products,
         tc.tile_pool(name="acts", bufs=2) as acts,
         tc.tile_pool(name="results", bufs=OUT_BANKS) as results,
-        tc.psum_pool(name="node_psum", bufs=2) as node_psum,
-        tc.psum_pool(name="head_psum", bufs=2) as head_psum,
+        tc.psum_pool(name="node_psum", bufs=1) as node_psum,
+        tc.psum_pool(name="head_psum", bufs=1) as head_psum,
         tc.psum_pool(name="joint_psum", bufs=1) as joint_psum,
     ):
         offsets = held.tile([P, LIST // 16], U16, name="offsets")
@@ -81,24 +79,31 @@ def tile_lcnchannelstack_b_kernel(
         def row_blocks(matrix):
             return matrix.rearrange("(a p) o -> p a o", p=P)
 
-        half = IN_NODES // 2
-        loads = [(x_tiles[0][:, :half], x_rows(0)[:, :half]), (x_tiles[0][:, half:], x_rows(0)[:, half:])]
-        loads.extend((w_tiles[0][0][:, start : start + width], repeated(wp, start, width)) for start, width in cuts(0, 0))
+        middle = IN_NODES // 2
+        loads = [(x_tiles[0][:, :middle], x_rows(0)[:, :middle]), (x_tiles[0][:, middle:], x_rows(0)[:, middle:])]
+        first_cuts = [(sum(FIRST_CUTS[:i]), entries) for i, entries in enumerate(FIRST_CUTS)]
+        loads.extend(
+            (w_tiles[0][0][:, first : first + entries], repeated(wp, first, entries)) for first, entries in first_cuts
+        )
         loads.extend((w_tiles[0][j][:], repeated(wp, j * PIECE, PIECE)) for j in range(1, PIECES))
-        loads.append((x_tiles[1][:], x_rows(1)))
-        loads.extend((w_tiles[1][j][:], repeated(wn, j * PIECE, PIECE)) for j in range(PIECES))
         loads.extend(
             [
                 (node_bias[0][:], column(bp)),
                 (head_bias[0][:], column(fcp_b)),
+                (node_bias[1][:], column(bn)),
+                (head_bias[1][:], column(fcn_b)),
+                (joint_bias[:], column(fc3_b)),
+            ]
+        )
+        loads.append((x_tiles[1][:], x_rows(1)))
+        loads.extend((w_tiles[1][j][:], repeated(wn, j * PIECE, PIECE)) for j in range(PIECES))
+        loads.extend(
+            [
                 (head_w[0][:], row_blocks(fcp_w)),
                 (joint_w[:, :HEAD_BLOCKS, :], row_blocks(fc3_w[:HEAD, :])),
                 (x_tiles[2][:], x_rows(2)),
-                (node_bias[1][:], column(bn)),
-                (head_bias[1][:], column(fcn_b)),
                 (head_w[1][:], row_blocks(fcn_w)),
                 (joint_w[:, HEAD_BLOCKS:, :], row_blocks(fc3_w[HEAD:, :])),
-                (joint_bias[:], column(fc3_b)),
             ]
         )
         loads.extend((x_tiles[s][:], x_rows(s)) for s in range(3, STEPS))
@@ -110,62 +115,71 @@ def tile_lcnchannelstack_b_kernel(
 
         node_sums = {}
         hidden = {}
+        head_sums = {}
         joint_in = {}
         joint_sums = {}
 
-        def look_up(s, j):
-            if j == 0:
-                node_sums[s] = node_psum.tile([P, NODE_BLOCKS, P], F32, name="node_sum")
-            for start, width in cuts(s, j):
-                first = j * PIECE + start
-                prod = products.tile([P, PIECE], F32, name="prod")
-                nc.vector.tensor_tensor(
-                    prod[:, :width],
-                    x_tiles[s][:].indirect(offsets[:, first // 16 : (first + width) // 16]),
-                    w_tiles[s % CHANNELS][j][:, start : start + width],
-                    MULT,
-                )
-                for i in range(width // P):
-                    entry = first + i * P
-                    nc.tensor.matmul(
-                        node_sums[s][:, entry // P % NODE_BLOCKS, :],
-                        lhsT=prod[:, i * P : (i + 1) * P],
-                        rhs=identity[:],
-                        is_transpose=True,
-                        start=(entry == 0),
-                        stop=(entry == LIST - P),
-                    )
 
-        def activate_nodes(s):
-            hidden[s] = acts.tile([P, NODE_BLOCKS, P], BF16, name="hidden")
-            for a in range(NODE_BLOCKS):
+        def look_up(s, first, entries):
+            if first == 0:
+                node_sums[s] = [
+                    node_psum.tile([P, HALF_BLOCKS, P], F32, name=f"node_sum{h}") for h in range(NODE_HALVES)
+                ]
+            prod = products.tile([P, PIECE], F32, name="prod")
+            nc.vector.tensor_tensor(
+                prod[:, :entries],
+                x_tiles[s][:].indirect(offsets[:, first // 16 : (first + entries) // 16]),
+                w_tiles[s % CHANNELS][first // PIECE][:, first % PIECE : first % PIECE + entries],
+                MULT,
+            )
+            for i in range(entries // P):
+                neighbour, a = divmod(first // P + i, NODE_BLOCKS)
+                nc.tensor.matmul(
+                    node_sums[s][a // HALF_BLOCKS][:, a % HALF_BLOCKS, :],
+                    lhsT=prod[:, i * P : (i + 1) * P],
+                    rhs=identity[:],
+                    is_transpose=True,
+                    start=(neighbour == 0 and a % HALF_BLOCKS == 0),
+                    stop=(neighbour == NEIGHBOURS - 1 and a % HALF_BLOCKS == HALF_BLOCKS - 1),
+                )
+
+        def activate_nodes(s, h):
+            if h == 0:
+                hidden[s] = acts.tile([P, NODE_BLOCKS, P], BF16, name="hidden")
+            for a in range(h * HALF_BLOCKS, (h + 1) * HALF_BLOCKS):
                 nc.scalar.activation(
                     hidden[s][:, a, :],
-                    node_sums[s][:, a, :],
+                    node_sums[s][h][:, a % HALF_BLOCKS, :],
                     RELU,
                     bias=node_bias[s % CHANNELS][:, a : a + 1],
                 )
 
-        def head_bank(s, bank):
+        def head_part(s, h):
             c, pair = s % CHANNELS, s // CHANNELS
-            if c == 0 and bank == 0:
+            if h == 0:
+                head_sums[s] = [head_psum.tile([P, FULL_BANK, P], F32, name=f"head_sum{b}") for b in range(HEAD_BANKS)]
+            if h == NODE_HALVES - 1 and c == 0:
                 joint_in[pair] = acts.tile([P, JOINT_BLOCKS, P], BF16, name="joint_in")
-            y = head_psum.tile([P, FULL_BANK, P], F32, name="y")
-            for a in range(NODE_BLOCKS):
-                for i in range(FULL_BANK):
-                    m = bank * FULL_BANK + i
-                    nc.tensor.matmul(
-                        y[:, i, :],
-                        lhsT=head_w[c][:, a, m * P : (m + 1) * P],
-                        rhs=hidden[s][:, a, :],
-                        start=(a == 0 and i == 0),
-                        stop=(a == NODE_BLOCKS - 1 and i == FULL_BANK - 1),
-                    )
-            for i in range(FULL_BANK):
-                m = bank * FULL_BANK + i
-                nc.scalar.activation(
-                    joint_in[pair][:, c * HEAD_BLOCKS + m, :], y[:, i, :], RELU, bias=head_bias[c][:, m : m + 1]
-                )
+            for b in range(HEAD_BANKS):
+                for a in range(h * HALF_BLOCKS, (h + 1) * HALF_BLOCKS):
+                    for i in range(FULL_BANK):
+                        m = b * FULL_BANK + i
+                        nc.tensor.matmul(
+                            head_sums[s][b][:, i, :],
+                            lhsT=head_w[c][:, a, m * P : (m + 1) * P],
+                            rhs=hidden[s][:, a, :],
+                            start=(a == 0 and i == 0),
+                            stop=(a == NODE_BLOCKS - 1 and i == FULL_BANK - 1),
+                        )
+                if h == NODE_HALVES - 1:
+                    for i in range(FULL_BANK):
+                        m = b * FULL_BANK + i
+                        nc.scalar.activation(
+                            joint_in[pair][:, c * HEAD_BLOCKS + m, :],
+                            head_sums[s][b][:, i, :],
+                            RELU,
+                            bias=head_bias[c][:, m : m + 1],
+                        )
 
         def joint_part(s, e_in_head, banks):
             c, pair = s % CHANNELS, s // CHANNELS
@@ -194,34 +208,52 @@ def tile_lcnchannelstack_b_kernel(
             of_bank = slice(bank * BANK_BLOCKS, (bank + 1) * BANK_BLOCKS)
             nc.sync.dma_start(out_blocks[:, of_bank, pair * P : (pair + 1) * P], result[:])
 
-        def dense_share(s, j):
+        def joint_share(s, q):
             pair = s // CHANNELS
-            first_joint = PIECES - OUT_BANKS
-            first_head = first_joint - HEAD_BANKS
-            if first_head <= j < first_joint:
-                head_bank(s, j - first_head)
-            elif j >= first_joint and s % CHANNELS < CHANNELS - 1:
-                quarter = HEAD_BLOCKS // OUT_BANKS
-                for e_in_head in range((j - first_joint) * quarter, (j - first_joint + 1) * quarter):
+            if s % CHANNELS < CHANNELS - 1:
+                blocks = HEAD_BLOCKS // OUT_BANKS
+                for e_in_head in range(q * blocks, (q + 1) * blocks):
                     joint_part(s, e_in_head, range(OUT_BANKS))
-            elif first_joint <= j < first_joint + EARLY_BANKS:
-                half = HEAD_BLOCKS // EARLY_BANKS
-                for e_in_head in range((j - first_joint) * half, (j - first_joint + 1) * half):
+            elif q < EARLY_BANKS:
+                blocks = HEAD_BLOCKS // EARLY_BANKS
+                for e_in_head in range(q * blocks, (q + 1) * blocks):
                     joint_part(s, e_in_head, range(EARLY_BANKS))
-                if j == first_joint + EARLY_BANKS - 1:
+                if q == EARLY_BANKS - 1:
                     for bank in range(EARLY_BANKS):
                         store_bank(pair, bank)
-            elif j >= first_joint + EARLY_BANKS:
-                bank = j - first_joint
+            else:
                 for e_in_head in range(HEAD_BLOCKS):
-                    joint_part(s, e_in_head, range(bank, bank + 1))
-                store_bank(pair, bank)
+                    joint_part(s, e_in_head, range(q, q + 1))
+                store_bank(pair, q)
 
-        for s in range(STEPS + 1):
+        def dense_share(s, share):
+            if share < NODE_HALVES:
+                head_part(s, share)
+            else:
+                joint_share(s, share - NODE_HALVES)
+
+        last = STEPS - 1
+        shares = NODE_HALVES + OUT_BANKS
+        for s in range(STEPS):
             for j in range(PIECES):
-                if s < STEPS:
-                    look_up(s, j)
-                if s > 0:
-                    dense_share(s - 1, j)
-            if s < STEPS:
-                activate_nodes(s)
+                if s > 0 and j >= PIECES - shares and (s < last or j < PIECES - 1):
+                    dense_share(s - 1, j - (PIECES - shares))
+                if (s, j) == (0, 0):
+                    for first, entries in first_cuts:
+                        look_up(s, first, entries)
+                elif s < last or j < PIECES - FINE_PIECES:
+                    look_up(s, j * PIECE, PIECE)
+            if s < last:
+                for h in range(NODE_HALVES):
+                    activate_nodes(s, h)
+
+        half_nodes = OUT_NODES // NODE_HALVES
+        for h in range(NODE_HALVES):
+            for neighbour in range(NEIGHBOURS - FINE_NEIGHBOURS, NEIGHBOURS):
+                look_up(last, neighbour * OUT_NODES + h * half_nodes, half_nodes)
+            activate_nodes(last, h)
+            if h == 0:
+                dense_share(last - 1, shares - 1)
+            head_part(last, h)
+        for q in range(OUT_BANKS):
+            joint_share(last, q)

@@ -80,11 +80,13 @@ def tile_lcnchannelstack_b_kernel(
             return matrix.rearrange("(a p) o -> p a o", p=P)
 
         middle = IN_NODES // 2
-        loads = [(x_tiles[0][:, :middle], x_rows(0)[:, :middle]), (x_tiles[0][:, middle:], x_rows(0)[:, middle:])]
         first_cuts = [(sum(FIRST_CUTS[:i]), entries) for i, entries in enumerate(FIRST_CUTS)]
-        loads.extend(
+        cut_loads = [
             (w_tiles[0][0][:, first : first + entries], repeated(wp, first, entries)) for first, entries in first_cuts
-        )
+        ]
+        loads = cut_loads[:1]
+        loads.extend([(x_tiles[0][:, :middle], x_rows(0)[:, :middle]), (x_tiles[0][:, middle:], x_rows(0)[:, middle:])])
+        loads.extend(cut_loads[1:])
         loads.extend((w_tiles[0][j][:], repeated(wp, j * PIECE, PIECE)) for j in range(1, PIECES))
         loads.extend(
             [

@@ -19,8 +19,6 @@ CHANNELS = 2
 
 PIECE = 1024
 PIECES = LIST // PIECE
-FIRST_CUTS = (256, 256, 512)
-assert sum(FIRST_CUTS) == PIECE
 NODE_HALVES = 2
 FINE_NEIGHBOURS = 6
 FINE_PIECES = FINE_NEIGHBOURS * OUT_NODES // PIECE
@@ -79,14 +77,7 @@ def tile_lcnchannelstack_b_kernel(
         def row_blocks(matrix):
             return matrix.rearrange("(a p) o -> p a o", p=P)
 
-        middle = IN_NODES // 2
-        first_cuts = [(sum(FIRST_CUTS[:i]), entries) for i, entries in enumerate(FIRST_CUTS)]
-        cut_loads = [
-            (w_tiles[0][0][:, first : first + entries], repeated(wp, first, entries)) for first, entries in first_cuts
-        ]
-        loads = cut_loads[:1]
-        loads.extend([(x_tiles[0][:, :middle], x_rows(0)[:, :middle]), (x_tiles[0][:, middle:], x_rows(0)[:, middle:])])
-        loads.extend(cut_loads[1:])
+        loads = [(w_tiles[0][0][:], repeated(wp, 0, PIECE)), (x_tiles[0][:], x_rows(0))]
         loads.extend((w_tiles[0][j][:], repeated(wp, j * PIECE, PIECE)) for j in range(1, PIECES))
         loads.extend(
             [
@@ -240,10 +231,7 @@ def tile_lcnchannelstack_b_kernel(
             for j in range(PIECES):
                 if s > 0 and j >= PIECES - shares and (s < last or j < PIECES - 1):
                     dense_share(s - 1, j - (PIECES - shares))
-                if (s, j) == (0, 0):
-                    for first, entries in first_cuts:
-                        look_up(s, first, entries)
-                elif s < last or j < PIECES - FINE_PIECES:
+                if s < last or j < PIECES - FINE_PIECES:
                     look_up(s, j * PIECE, PIECE)
             if s < last:
                 for h in range(NODE_HALVES):

@@ -103,8 +103,8 @@ def tile_lcnchannelstack_b_kernel(
 
         nc.sync.dma_start(offsets[:], offs)
         with nc.allow_non_contiguous_dma(reason="bias vectors, one float32 to a partition"):
-            for i, (part, source) in enumerate(loads):
-                (nc.scalar, nc.sync)[i % 2].dma_start(part, source)
+            for part, source in loads:
+                nc.sync.dma_start(part, source)
 
         node_sums = {}
         hidden = {}

@@ -30,7 +30,8 @@ HALF_BLOCKS = NODE_BLOCKS // NODE_HALVES
 FULL_BANK = 4
 HEAD_BANKS = HEAD_BLOCKS // FULL_BANK
 OUT_BANKS = 4
-BANK_BLOCKS = HEAD_BLOCKS // OUT_BANKS
+BANK_WIDTHS = (2, 2, 3, 1)
+BANK_FIRST = tuple(sum(BANK_WIDTHS[:bank]) for bank in range(OUT_BANKS))
 EARLY_BANKS = OUT_BANKS // 2
 
 FLOPS = 2 * CHANNELS * SAMPLES * LIST + 2 * SAMPLES * (CHANNELS * OUT_NODES * HEAD + CHANNELS * HEAD * HEAD)
@@ -92,9 +93,9 @@ def tile_lcnchannelstack_b_kernel(
         loads.extend((w_tiles[1][j][:], repeated(wn, j * PIECE, PIECE)) for j in range(PIECES))
         loads.extend(
             [
+                (x_tiles[2][:], x_rows(2)),
                 (head_w[0][:], row_blocks(fcp_w)),
                 (joint_w[:, :HEAD_BLOCKS, :], row_blocks(fc3_w[:HEAD, :])),
-                (x_tiles[2][:], x_rows(2)),
                 (head_w[1][:], row_blocks(fcn_w)),
                 (joint_w[:, HEAD_BLOCKS:, :], row_blocks(fc3_w[HEAD:, :])),
             ]
@@ -179,27 +180,30 @@ def tile_lcnchannelstack_b_kernel(
             e = c * HEAD_BLOCKS + e_in_head
             if e == 0:
                 joint_sums[pair] = [
-                    joint_psum.tile([P, BANK_BLOCKS, P], F32, name=f"joint_sum{bank}") for bank in range(OUT_BANKS)
+                    joint_psum.tile([P, FULL_BANK, P], F32, name=f"joint_sum{bank}") for bank in range(OUT_BANKS)
                 ]
-            for m in range(banks.start * BANK_BLOCKS, banks.stop * BANK_BLOCKS):
-                nc.tensor.matmul(
-                    joint_sums[pair][m // BANK_BLOCKS][:, m % BANK_BLOCKS, :],
-                    lhsT=joint_w[:, e, m * P : (m + 1) * P],
-                    rhs=joint_in[pair][:, e, :],
-                    start=(e == 0 and m % BANK_BLOCKS == 0),
-                    stop=(e == JOINT_BLOCKS - 1 and m % BANK_BLOCKS == BANK_BLOCKS - 1),
-                )
+            for bank in banks:
+                for i in range(BANK_WIDTHS[bank]):
+                    m = BANK_FIRST[bank] + i
+                    nc.tensor.matmul(
+                        joint_sums[pair][bank][:, i, :],
+                        lhsT=joint_w[:, e, m * P : (m + 1) * P],
+                        rhs=joint_in[pair][:, e, :],
+                        start=(e == 0 and i == 0),
+                        stop=(e == JOINT_BLOCKS - 1 and i == BANK_WIDTHS[bank] - 1),
+                    )
 
         def store_bank(pair, bank):
             out_blocks = out.rearrange("(m p) r -> p m r", p=P)
-            result = results.tile([P, BANK_BLOCKS, P], F32, name="result")
-            for i in range(BANK_BLOCKS):
-                m = bank * BANK_BLOCKS + i
+            width = BANK_WIDTHS[bank]
+            result = results.tile([P, max(BANK_WIDTHS), P], F32, name="result")
+            for i in range(width):
+                m = BANK_FIRST[bank] + i
                 nc.scalar.activation(
                     result[:, i, :], joint_sums[pair][bank][:, i, :], IDENTITY, bias=joint_bias[:, m : m + 1]
                 )
-            of_bank = slice(bank * BANK_BLOCKS, (bank + 1) * BANK_BLOCKS)
-            nc.sync.dma_start(out_blocks[:, of_bank, pair * P : (pair + 1) * P], result[:])
+            of_bank = slice(BANK_FIRST[bank], BANK_FIRST[bank] + width)
+            nc.sync.dma_start(out_blocks[:, of_bank, pair * P : (pair + 1) * P], result[:, :width, :])
 
         def joint_share(s, q):
             pair = s // CHANNELS

@@ -43,7 +43,7 @@ def tile_lcnchannelstack_b_kernel(
     nc = tc.nc
     with (
         tc.tile_pool(name="held", bufs=1) as held,
-        tc.tile_pool(name="products", bufs=10) as products,
+        tc.tile_pool(name="products", bufs=16) as products,
         tc.tile_pool(name="acts", bufs=2) as acts,
         tc.tile_pool(name="results", bufs=OUT_BANKS) as results,
         tc.psum_pool(name="node_psum", bufs=1) as node_psum,

@@ -19,20 +19,22 @@ CHANNELS = 2
 
 PIECE = 1024
 PIECES = LIST // PIECE
-NODE_HALVES = 2
+NODE_BLOCKS = OUT_NODES // P
+PART_BLOCKS = (range(0, 2), range(2, 3), range(3, 4))
+NODE_PARTS = len(PART_BLOCKS)
 FINE_NEIGHBOURS = 6
 FINE_PIECES = FINE_NEIGHBOURS * OUT_NODES // PIECE
-NODE_BLOCKS = OUT_NODES // P
 HEAD_BLOCKS = HEAD // P
 JOINT_BLOCKS = CHANNELS * HEAD_BLOCKS
 STEPS = CHANNELS * SAMPLES // P
-HALF_BLOCKS = NODE_BLOCKS // NODE_HALVES
 FULL_BANK = 4
 HEAD_BANKS = HEAD_BLOCKS // FULL_BANK
-OUT_BANKS = 4
-BANK_WIDTHS = (2, 2, 3, 1)
+OUT_BANKS = 3
+BANK_WIDTHS = (4, 3, 1)
 BANK_FIRST = tuple(sum(BANK_WIDTHS[:bank]) for bank in range(OUT_BANKS))
-EARLY_BANKS = OUT_BANKS // 2
+HEAD_SHARES = 2
+JOINT_SHARES = 4
+EARLY_SHARES = JOINT_SHARES - (OUT_BANKS - 1)
 
 FLOPS = 2 * CHANNELS * SAMPLES * LIST + 2 * SAMPLES * (CHANNELS * OUT_NODES * HEAD + CHANNELS * HEAD * HEAD)
 
@@ -117,7 +119,7 @@ def tile_lcnchannelstack_b_kernel(
         def look_up(s, first, entries):
             if first == 0:
                 node_sums[s] = [
-                    node_psum.tile([P, HALF_BLOCKS, P], F32, name=f"node_sum{h}") for h in range(NODE_HALVES)
+                    node_psum.tile([P, FULL_BANK, P], F32, name=f"node_sum{part}") for part in range(NODE_PARTS)
                 ]
             prod = products.tile([P, PIECE], F32, name="prod")
             nc.vector.tensor_tensor(
@@ -128,34 +130,36 @@ def tile_lcnchannelstack_b_kernel(
             )
             for i in range(entries // P):
                 neighbour, a = divmod(first // P + i, NODE_BLOCKS)
+                part = [a in blocks for blocks in PART_BLOCKS].index(True)
+                blocks = PART_BLOCKS[part]
                 nc.tensor.matmul(
-                    node_sums[s][a // HALF_BLOCKS][:, a % HALF_BLOCKS, :],
+                    node_sums[s][part][:, a - blocks.start, :],
                     lhsT=prod[:, i * P : (i + 1) * P],
                     rhs=identity[:],
                     is_transpose=True,
-                    start=(neighbour == 0 and a % HALF_BLOCKS == 0),
-                    stop=(neighbour == NEIGHBOURS - 1 and a % HALF_BLOCKS == HALF_BLOCKS - 1),
+                    start=(neighbour == 0 and a == blocks.start),
+                    stop=(neighbour == NEIGHBOURS - 1 and a == blocks.stop - 1),
                 )
 
-        def activate_nodes(s, h):
-            if h == 0:
+        def activate_nodes(s, part):
+            if part == 0:
                 hidden[s] = acts.tile([P, NODE_BLOCKS, P], BF16, name="hidden")
-            for a in range(h * HALF_BLOCKS, (h + 1) * HALF_BLOCKS):
+            for a in PART_BLOCKS[part]:
                 nc.scalar.activation(
                     hidden[s][:, a, :],
-                    node_sums[s][h][:, a % HALF_BLOCKS, :],
+                    node_sums[s][part][:, a - PART_BLOCKS[part].start, :],
                     RELU,
                     bias=node_bias[s % CHANNELS][:, a : a + 1],
                 )
 
-        def head_part(s, h):
+        def head_part(s, part):
             c, pair = s % CHANNELS, s // CHANNELS
-            if h == 0:
+            if part == 0:
                 head_sums[s] = [head_psum.tile([P, FULL_BANK, P], F32, name=f"head_sum{b}") for b in range(HEAD_BANKS)]
-            if h == NODE_HALVES - 1 and c == 0:
+            if part == NODE_PARTS - 1 and c == 0:
                 joint_in[pair] = acts.tile([P, JOINT_BLOCKS, P], BF16, name="joint_in")
             for b in range(HEAD_BANKS):
-                for a in range(h * HALF_BLOCKS, (h + 1) * HALF_BLOCKS):
+                for a in PART_BLOCKS[part]:
                     for i in range(FULL_BANK):
                         m = b * FULL_BANK + i
                         nc.tensor.matmul(
@@ -165,7 +169,7 @@ def tile_lcnchannelstack_b_kernel(
                             start=(a == 0 and i == 0),
                             stop=(a == NODE_BLOCKS - 1 and i == FULL_BANK - 1),
                         )
-                if h == NODE_HALVES - 1:
+                if part == NODE_PARTS - 1:
                     for i in range(FULL_BANK):
                         m = b * FULL_BANK + i
                         nc.scalar.activation(
@@ -208,29 +212,32 @@ def tile_lcnchannelstack_b_kernel(
         def joint_share(s, q):
             pair = s // CHANNELS
             if s % CHANNELS < CHANNELS - 1:
-                blocks = HEAD_BLOCKS // OUT_BANKS
+                blocks = HEAD_BLOCKS // JOINT_SHARES
                 for e_in_head in range(q * blocks, (q + 1) * blocks):
                     joint_part(s, e_in_head, range(OUT_BANKS))
-            elif q < EARLY_BANKS:
-                blocks = HEAD_BLOCKS // EARLY_BANKS
+            elif q < EARLY_SHARES:
+                blocks = HEAD_BLOCKS // EARLY_SHARES
                 for e_in_head in range(q * blocks, (q + 1) * blocks):
-                    joint_part(s, e_in_head, range(EARLY_BANKS))
-                if q == EARLY_BANKS - 1:
-                    for bank in range(EARLY_BANKS):
-                        store_bank(pair, bank)
+                    joint_part(s, e_in_head, range(1))
+                if q == EARLY_SHARES - 1:
+                    store_bank(pair, 0)
             else:
+                bank = q - EARLY_SHARES + 1
                 for e_in_head in range(HEAD_BLOCKS):
-                    joint_part(s, e_in_head, range(q, q + 1))
-                store_bank(pair, q)
+                    joint_part(s, e_in_head, range(bank, bank + 1))
+                store_bank(pair, bank)
 
         def dense_share(s, share):
-            if share < NODE_HALVES:
-                head_part(s, share)
+            if share == 0:
+                head_part(s, 0)
+            elif share == 1:
+                for part in range(1, NODE_PARTS):
+                    head_part(s, part)
             else:
-                joint_share(s, share - NODE_HALVES)
+                joint_share(s, share - HEAD_SHARES)
 
         last = STEPS - 1
-        shares = NODE_HALVES + OUT_BANKS
+        shares = HEAD_SHARES + JOINT_SHARES
         for s in range(STEPS):
             for j in range(PIECES):
                 if s > 0 and j >= PIECES - shares and (s < last or j < PIECES - 1):
@@ -238,16 +245,23 @@ def tile_lcnchannelstack_b_kernel(
                 if s < last or j < PIECES - FINE_PIECES:
                     look_up(s, j * PIECE, PIECE)
             if s < last:
-                for h in range(NODE_HALVES):
-                    activate_nodes(s, h)
+                for part in range(NODE_PARTS):
+                    activate_nodes(s, part)
 
-        half_nodes = OUT_NODES // NODE_HALVES
-        for h in range(NODE_HALVES):
-            for neighbour in range(NEIGHBOURS - FINE_NEIGHBOURS, NEIGHBOURS):
-                look_up(last, neighbour * OUT_NODES + h * half_nodes, half_nodes)
-            activate_nodes(last, h)
-            if h == 0:
-                dense_share(last - 1, shares - 1)
-            head_part(last, h)
-        for q in range(OUT_BANKS):
+        fine = range(NEIGHBOURS - FINE_NEIGHBOURS, NEIGHBOURS)
+        half_nodes = OUT_NODES // 2
+        for neighbour in fine:
+            look_up(last, neighbour * OUT_NODES, half_nodes)
+        activate_nodes(last, 0)
+        dense_share(last - 1, shares - 1)
+        head_part(last, 0)
+        for neighbour in fine:
+            if neighbour < NEIGHBOURS - 1:
+                look_up(last, neighbour * OUT_NODES + half_nodes, half_nodes)
+        for part in range(1, NODE_PARTS):
+            look_up(last, (NEIGHBOURS - 1) * OUT_NODES + PART_BLOCKS[part].start * P, len(PART_BLOCKS[part]) * P)
+            activate_nodes(last, part)
+        for part in range(1, NODE_PARTS):
+            head_part(last, part)
+        for q in range(JOINT_SHARES):
             joint_share(last, q)

@@ -239,9 +239,10 @@ def tile_lcnchannelstack_b_kernel(
         last = STEPS - 1
         shares = HEAD_SHARES + JOINT_SHARES
         for s in range(STEPS):
+            first_share = PIECES - shares - (1 if s == last else 0)
             for j in range(PIECES):
-                if s > 0 and j >= PIECES - shares and (s < last or j < PIECES - 1):
-                    dense_share(s - 1, j - (PIECES - shares))
+                if s > 0 and first_share <= j < first_share + shares - (1 if s == last else 0):
+                    dense_share(s - 1, j - first_share)
                 if s < last or j < PIECES - FINE_PIECES:
                     look_up(s, j * PIECE, PIECE)
             if s < last:
@@ -255,13 +256,18 @@ def tile_lcnchannelstack_b_kernel(
         activate_nodes(last, 0)
         dense_share(last - 1, shares - 1)
         head_part(last, 0)
+        blockwise = range(NEIGHBOURS - 3, NEIGHBOURS)
         for neighbour in fine:
-            if neighbour < NEIGHBOURS - 1:
+            if neighbour not in blockwise:
                 look_up(last, neighbour * OUT_NODES + half_nodes, half_nodes)
-        for part in range(1, NODE_PARTS):
-            look_up(last, (NEIGHBOURS - 1) * OUT_NODES + PART_BLOCKS[part].start * P, len(PART_BLOCKS[part]) * P)
-            activate_nodes(last, part)
-        for part in range(1, NODE_PARTS):
-            head_part(last, part)
+        for neighbour in blockwise:
+            look_up(last, neighbour * OUT_NODES + PART_BLOCKS[1].start * P, P)
+        activate_nodes(last, 1)
+        for neighbour in blockwise:
+            if neighbour == NEIGHBOURS - 1:
+                head_part(last, 1)
+            look_up(last, neighbour * OUT_NODES + PART_BLOCKS[2].start * P, P)
+        activate_nodes(last, 2)
+        head_part(last, 2)
         for q in range(JOINT_SHARES):
             joint_share(last, q)

@@ -5,6 +5,8 @@ F32 = mybir.dt.float32
 BF16 = mybir.dt.bfloat16
 U16 = mybir.dt.uint16
 MULT = mybir.AluOpType.mult
+ADD = mybir.AluOpType.add
+MAX = mybir.AluOpType.max
 RELU = mybir.ActivationFunctionType.Relu
 IDENTITY = mybir.ActivationFunctionType.Identity
 
@@ -116,6 +118,14 @@ def tile_lcnchannelstack_b_kernel(
         joint_sums = {}
 
 
+        def leave_psum(target, sums, bias, relu, by_vector):
+            if by_vector and relu:
+                nc.vector.tensor_scalar(target, sums, bias, 0.0, op0=ADD, op1=MAX)
+            elif by_vector:
+                nc.vector.tensor_scalar(target, sums, bias, None, op0=ADD)
+            else:
+                nc.scalar.activation(target, sums, RELU if relu else IDENTITY, bias=bias)
+
         def look_up(s, first, entries):
             if first == 0:
                 node_sums[s] = [
@@ -172,11 +182,12 @@ def tile_lcnchannelstack_b_kernel(
                 if part == NODE_PARTS - 1:
                     for i in range(FULL_BANK):
                         m = b * FULL_BANK + i
-                        nc.scalar.activation(
+                        leave_psum(
                             joint_in[pair][:, c * HEAD_BLOCKS + m, :],
                             head_sums[s][b][:, i, :],
-                            RELU,
-                            bias=head_bias[c][:, m : m + 1],
+                            head_bias[c][:, m : m + 1],
+                            relu=True,
+                            by_vector=(s == STEPS - 1 and b % 2 == 1),
                         )
 
         def joint_part(s, e_in_head, banks):
@@ -203,8 +214,12 @@ def tile_lcnchannelstack_b_kernel(
             result = results.tile([P, max(BANK_WIDTHS), P], F32, name="result")
             for i in range(width):
                 m = BANK_FIRST[bank] + i
-                nc.scalar.activation(
-                    result[:, i, :], joint_sums[pair][bank][:, i, :], IDENTITY, bias=joint_bias[:, m : m + 1]
+                leave_psum(
+                    result[:, i, :],
+                    joint_sums[pair][bank][:, i, :],
+                    joint_bias[:, m : m + 1],
+                    relu=False,
+                    by_vector=(pair == STEPS // CHANNELS - 1 and bank % 2 == 1),
                 )
             of_bank = slice(BANK_FIRST[bank], BANK_FIRST[bank] + width)
             nc.sync.dma_start(out_blocks[:, of_bank, pair * P : (pair + 1) * P], result[:, :width, :])

import concourse.mybir as mybir
from concourse.masks import make_identity

F32 = mybir.dt.float32
BF16 = mybir.dt.bfloat16
U16 = mybir.dt.uint16
MULT = mybir.AluOpType.mult
ADD = mybir.AluOpType.add
MAX = mybir.AluOpType.max
RELU = mybir.ActivationFunctionType.Relu
IDENTITY = mybir.ActivationFunctionType.Identity

P = 128
SAMPLES = 512
IN_NODES = 1024
OUT_NODES = 512
NEIGHBOURS = 16
LIST = NEIGHBOURS * OUT_NODES
HEAD = 1024
CHANNELS = 2

PIECE = 1024
PIECES = LIST // PIECE
NODE_BLOCKS = OUT_NODES // P
PART_BLOCKS = (range(0, 2), range(2, 3), range(3, 4))
NODE_PARTS = len(PART_BLOCKS)
FINE_NEIGHBOURS = 6
FINE_PIECES = FINE_NEIGHBOURS * OUT_NODES // PIECE
HEAD_BLOCKS = HEAD // P
JOINT_BLOCKS = CHANNELS * HEAD_BLOCKS
STEPS = CHANNELS * SAMPLES // P
FULL_BANK = 4
HEAD_BANKS = HEAD_BLOCKS // FULL_BANK
OUT_BANKS = 3
BANK_WIDTHS = (4, 3, 1)
BANK_FIRST = tuple(sum(BANK_WIDTHS[:bank]) for bank in range(OUT_BANKS))
HEAD_SHARES = 2
JOINT_SHARES = 4
EARLY_SHARES = JOINT_SHARES - (OUT_BANKS - 1)

FLOPS = 2 * CHANNELS * SAMPLES * LIST + 2 * SAMPLES * (CHANNELS * OUT_NODES * HEAD + CHANNELS * HEAD * HEAD)


def tile_lcnchannelstack_b_kernel(
    tc, x, wp, wn, bp, bn, fcp_w, fcp_b, fcn_w, fcn_b, fc3_w, fc3_b, offs, out
):
    nc = tc.nc
    with (
        tc.tile_pool(name="held", bufs=1) as held,
        tc.tile_pool(name="products", bufs=16) as products,
        tc.tile_pool(name="acts", bufs=2) as acts,
        tc.tile_pool(name="results", bufs=OUT_BANKS) as results,
        tc.psum_pool(name="node_psum", bufs=1) as node_psum,
        tc.psum_pool(name="head_psum", bufs=1) as head_psum,
        tc.psum_pool(name="joint_psum", bufs=1) as joint_psum,
    ):
        offsets = held.tile([P, LIST // 16], U16, name="offsets")
        identity = held.tile([P, P], F32, name="identity")
        x_tiles = [held.tile([P, IN_NODES], F32, name=f"x{s}") for s in range(STEPS)]
        w_tiles = [
            [held.tile([P, PIECE], F32, name=f"w{c}_{j}") for j in range(PIECES)]
            for c in range(CHANNELS)
        ]
        node_bias = [held.tile([P, NODE_BLOCKS], F32, name=f"node_bias{c}") for c in range(CHANNELS)]
        head_w = [held.tile([P, NODE_BLOCKS, HEAD], BF16, name=f"head_w{c}") for c in range(CHANNELS)]
        head_bias = [held.tile([P, HEAD_BLOCKS], F32, name=f"head_bias{c}") for c in range(CHANNELS)]
        joint_w = held.tile([P, JOINT_BLOCKS, HEAD], BF16, name="joint_w")
        joint_bias = held.tile([P, HEAD_BLOCKS], F32, name="joint_bias")

        make_identity(nc, identity[:])

        def x_rows(s):
            row = (s % CHANNELS) * SAMPLES + (s // CHANNELS) * P
            return x[row : row + P, :]

        def repeated(w, first, entries):
            return w.rearrange("o n -> (o n)")[first : first + entries].partition_broadcast(P)

        def column(vector):
            return vector.rearrange("(a p) o -> p (a o)", p=P)

        def row_blocks(matrix):
            return matrix.rearrange("(a p) o -> p a o", p=P)

        loads = [(w_tiles[0][0][:], repeated(wp, 0, PIECE)), (x_tiles[0][:], x_rows(0))]
        loads.extend((w_tiles[0][j][:], repeated(wp, j * PIECE, PIECE)) for j in range(1, PIECES))
        loads.extend(
            [
                (node_bias[0][:], column(bp)),
                (head_bias[0][:], column(fcp_b)),
                (node_bias[1][:], column(bn)),
                (head_bias[1][:], column(fcn_b)),
                (joint_bias[:], column(fc3_b)),
            ]
        )
        loads.append((x_tiles[1][:], x_rows(1)))
        loads.extend((w_tiles[1][j][:], repeated(wn, j * PIECE, PIECE)) for j in range(PIECES))
        loads.extend(
            [
                (x_tiles[2][:], x_rows(2)),
                (head_w[0][:], row_blocks(fcp_w)),
                (joint_w[:, :HEAD_BLOCKS, :], row_blocks(fc3_w[:HEAD, :])),
                (head_w[1][:], row_blocks(fcn_w)),
                (joint_w[:, HEAD_BLOCKS:, :], row_blocks(fc3_w[HEAD:, :])),
            ]
        )
        loads.extend((x_tiles[s][:], x_rows(s)) for s in range(3, STEPS))

        nc.sync.dma_start(offsets[:], offs)
        with nc.allow_non_contiguous_dma(reason="bias vectors, one float32 to a partition"):
            for part, source in loads:
                nc.sync.dma_start(part, source)

        node_sums = {}
        hidden = {}
        head_sums = {}
        joint_in = {}
        joint_sums = {}


        def leave_psum(target, sums, bias, relu, by_vector):
            if by_vector and relu:
                nc.vector.tensor_scalar(target, sums, bias, 0.0, op0=ADD, op1=MAX)
            elif by_vector:
                nc.vector.tensor_scalar(target, sums, bias, None, op0=ADD)
            else:
                nc.scalar.activation(target, sums, RELU if relu else IDENTITY, bias=bias)

        def look_up(s, first, entries):
            if first == 0:
                node_sums[s] = [
                    node_psum.tile([P, FULL_BANK, P], F32, name=f"node_sum{part}") for part in range(NODE_PARTS)
                ]
            prod = products.tile([P, PIECE], F32, name="prod")
            nc.vector.tensor_tensor(
                prod[:, :entries],
                x_tiles[s][:].indirect(offsets[:, first // 16 : (first + entries) // 16]),
                w_tiles[s % CHANNELS][first // PIECE][:, first % PIECE : first % PIECE + entries],
                MULT,
            )
            for i in range(entries // P):
                neighbour, a = divmod(first // P + i, NODE_BLOCKS)
                part = [a in blocks for blocks in PART_BLOCKS].index(True)
                blocks = PART_BLOCKS[part]
                nc.tensor.matmul(
                    node_sums[s][part][:, a - blocks.start, :],
                    lhsT=prod[:, i * P : (i + 1) * P],
                    rhs=identity[:],
                    is_transpose=True,
                    start=(neighbour == 0 and a == blocks.start),
                    stop=(neighbour == NEIGHBOURS - 1 and a == blocks.stop - 1),
                )

        def activate_nodes(s, part):
            if part == 0:
                hidden[s] = acts.tile([P, NODE_BLOCKS, P], BF16, name="hidden")
            for a in PART_BLOCKS[part]:
                nc.scalar.activation(
                    hidden[s][:, a, :],
                    node_sums[s][part][:, a - PART_BLOCKS[part].start, :],
                    RELU,
                    bias=node_bias[s % CHANNELS][:, a : a + 1],
                )

        def head_part(s, part):
            c, pair = s % CHANNELS, s // CHANNELS
            if part == 0:
                head_sums[s] = [head_psum.tile([P, FULL_BANK, P], F32, name=f"head_sum{b}") for b in range(HEAD_BANKS)]
            if part == NODE_PARTS - 1 and c == 0:
                joint_in[pair] = acts.tile([P, JOINT_BLOCKS, P], BF16, name="joint_in")
            for b in range(HEAD_BANKS):
                for a in PART_BLOCKS[part]:
                    for i in range(FULL_BANK):
                        m = b * FULL_BANK + i
                        nc.tensor.matmul(
                            head_sums[s][b][:, i, :],
                            lhsT=head_w[c][:, a, m * P : (m + 1) * P],
                            rhs=hidden[s][:, a, :],
                            start=(a == 0 and i == 0),
                            stop=(a == NODE_BLOCKS - 1 and i == FULL_BANK - 1),
                        )
                if part == NODE_PARTS - 1:
                    for i in range(FULL_BANK):
                        m = b * FULL_BANK + i
                        leave_psum(
                            joint_in[pair][:, c * HEAD_BLOCKS + m, :],
                            head_sums[s][b][:, i, :],
                            head_bias[c][:, m : m + 1],
                            relu=True,
                            by_vector=(s == STEPS - 1 and b % 2 == 1),
                        )

        def joint_part(s, e_in_head, banks):
            c, pair = s % CHANNELS, s // CHANNELS
            e = c * HEAD_BLOCKS + e_in_head
            if e == 0:
                joint_sums[pair] = [
                    joint_psum.tile([P, FULL_BANK, P], F32, name=f"joint_sum{bank}") for bank in range(OUT_BANKS)
                ]
            for bank in banks:
                for i in range(BANK_WIDTHS[bank]):
                    m = BANK_FIRST[bank] + i
                    nc.tensor.matmul(
                        joint_sums[pair][bank][:, i, :],
                        lhsT=joint_w[:, e, m * P : (m + 1) * P],
                        rhs=joint_in[pair][:, e, :],
                        start=(e == 0 and i == 0),
                        stop=(e == JOINT_BLOCKS - 1 and i == BANK_WIDTHS[bank] - 1),
                    )

        def store_bank(pair, bank):
            out_blocks = out.rearrange("(m p) r -> p m r", p=P)
            width = BANK_WIDTHS[bank]
            result = results.tile([P, max(BANK_WIDTHS), P], F32, name="result")
            for i in range(width):
                m = BANK_FIRST[bank] + i
                leave_psum(
                    result[:, i, :],
                    joint_sums[pair][bank][:, i, :],
                    joint_bias[:, m : m + 1],
                    relu=False,
                    by_vector=(pair == STEPS // CHANNELS - 1 and bank % 2 == 1),
                )
            of_bank = slice(BANK_FIRST[bank], BANK_FIRST[bank] + width)
            nc.sync.dma_start(out_blocks[:, of_bank, pair * P : (pair + 1) * P], result[:, :width, :])

        def joint_share(s, q):
            pair = s // CHANNELS
            if s % CHANNELS < CHANNELS - 1:
                blocks = HEAD_BLOCKS // JOINT_SHARES
                for e_in_head in range(q * blocks, (q + 1) * blocks):
                    joint_part(s, e_in_head, range(OUT_BANKS))
            elif q < EARLY_SHARES:
                blocks = HEAD_BLOCKS // EARLY_SHARES
                for e_in_head in range(q * blocks, (q + 1) * blocks):
                    joint_part(s, e_in_head, range(1))
                if q == EARLY_SHARES - 1:
                    store_bank(pair, 0)
            else:
                bank = q - EARLY_SHARES + 1
                for e_in_head in range(HEAD_BLOCKS):
                    joint_part(s, e_in_head, range(bank, bank + 1))
                store_bank(pair, bank)

        def dense_share(s, share):
            if share == 0:
                head_part(s, 0)
            elif share == 1:
                for part in range(1, NODE_PARTS):
                    head_part(s, part)
            else:
                joint_share(s, share - HEAD_SHARES)

        last = STEPS - 1
        shares = HEAD_SHARES + JOINT_SHARES
        for s in range(STEPS):
            first_share = PIECES - shares - (1 if s == last else 0)
            for j in range(PIECES):
                if s > 0 and first_share <= j < first_share + shares - (1 if s == last else 0):
                    dense_share(s - 1, j - first_share)
                if s < last or j < PIECES - FINE_PIECES:
                    look_up(s, j * PIECE, PIECE)
            if s < last:
                for part in range(NODE_PARTS):
                    activate_nodes(s, part)

        fine = range(NEIGHBOURS - FINE_NEIGHBOURS, NEIGHBOURS)
        half_nodes = OUT_NODES // 2
        for neighbour in fine:
            look_up(last, neighbour * OUT_NODES, half_nodes)
        activate_nodes(last, 0)
        dense_share(last - 1, shares - 1)
        head_part(last, 0)
        blockwise = range(NEIGHBOURS - 3, NEIGHBOURS)
        for neighbour in fine:
            if neighbour not in blockwise:
                look_up(last, neighbour * OUT_NODES + half_nodes, half_nodes)
        for neighbour in blockwise:
            look_up(last, neighbour * OUT_NODES + PART_BLOCKS[1].start * P, P)
        activate_nodes(last, 1)
        for neighbour in blockwise:
            if neighbour == NEIGHBOURS - 1:
                head_part(last, 1)
            look_up(last, neighbour * OUT_NODES + PART_BLOCKS[2].start * P, P)
        activate_nodes(last, 2)
        head_part(last, 2)
        for q in range(JOINT_SHARES):
            joint_share(last, q)
